import numpy as np
import ml_dtypes


def mxq(x, axis, fmt="e4m3"):
    dtype, down = {"e4m3": (ml_dtypes.float8_e4m3fn, 7), "e5m2": (ml_dtypes.float8_e5m2, 14)}[fmt]
    v = np.moveaxis(np.asarray(x, np.float32).astype(ml_dtypes.bfloat16).astype(np.float64), axis, -1)
    blocks = v.reshape(v.shape[:-1] + (-1, 32))
    amax = np.abs(blocks).max(-1, keepdims=True)
    byte = np.maximum(np.where(amax > 0, np.frexp(amax)[1] - 1 + 127, 0) - down, 1)
    scale = np.exp2(byte - 127.0)
    codes = (blocks / scale).astype(np.float32).astype(dtype).astype(np.float64)
    return np.moveaxis((codes * scale).reshape(v.shape), -1, axis)


WIDE = False


def mx_kscale(k):
    if not WIDE:
        return np.ones(k)
    levels = np.array([10, -10, 5, -5, 0])
    a = np.random.permutation(np.resize(levels, k // 512 * 4)).reshape(k // 512, 4)
    idx = np.arange(k)
    return np.exp2(a[idx // 512, idx % 128 // 32])


BF16 = ml_dtypes.bfloat16


def bf(x):
    return np.asarray(x, np.float32).astype(BF16)


def f64(x):
    return np.asarray(x).astype(np.float64)


N, C = 768, 512
KV = 2 * C
SQRT2 = np.sqrt(2.0)
EPS = 1e-6


def setup_inputs():
    t = mx_kscale(KV)
    return {"s": bf(np.random.standard_normal((N, C))),
            "v": bf(np.random.standard_normal((N, C, 3))),
            "g_v": bf(np.random.standard_normal((N, KV)) * t),
            "wv": bf(np.random.standard_normal((KV, C)) / t[:, None]),
            "ln_g1": bf(1.0 + 0.1 * np.random.standard_normal(C))}


def reference(s, v, g_v, wv, ln_g1):
    s, v = f64(s), f64(v)
    sv = SQRT2 * s[..., None] * v
    vec = np.concatenate([v, sv], axis=1) * f64(g_v)[..., None]
    dv = (mxq(vec.transpose(0, 2, 1), 2, "e4m3") @ mxq(f64(wv), 0, "e4m3")) / np.sqrt(KV)
    y = v + dv.transpose(0, 2, 1)
    rms = np.sqrt(np.mean(y * y, axis=(1, 2), keepdims=True) + EPS)
    return y / rms * f64(ln_g1)[None, :, None]

@@ -1,0 +1,230 @@
+from contextlib import ExitStack
+import math
+
+import concourse.mybir as mybir
+from concourse.masks import make_identity
+
+BF16 = mybir.dt.bfloat16
+F32 = mybir.dt.float32
+U32 = mybir.dt.uint32
+U8 = mybir.dt.uint8
+FP8X4 = mybir.dt.float8_e4m3fn_x4
+MULT = mybir.AluOpType.mult
+ADD = mybir.AluOpType.add
+ACT = mybir.ActivationFunctionType
+
+P = 128
+PACK = 4
+POINTS = 768
+C = 512
+DIMS = 3
+PASSES = 2
+TILES = POINTS // P
+EPS = 1e-6
+
+FLOPS = 2 * POINTS * DIMS * (PASSES * C) * C
+
+
+def tile_selfinteraction_pb_kernel(tc, s, v, g_v, wv, ln_g1, out):
+    nc = tc.nc
+    with ExitStack() as ctx:
+        const = ctx.enter_context(tc.tile_pool(name="const", bufs=1))
+        resident = ctx.enter_context(tc.tile_pool(name="resident", bufs=1))
+        work = ctx.enter_context(tc.tile_pool(name="work", bufs=2))
+        psum_t = ctx.enter_context(tc.psum_pool(name="psum_t", bufs=1))
+        psum_acc = ctx.enter_context(tc.psum_pool(name="psum_acc", bufs=5))
+        ctx.enter_context(tc.manual_schedule())
+
+        g_sb = [resident.tile([P, PASSES * PACK, P], BF16, name="g_sb%d" % i) for i in range(TILES)]
+        s_sb = [resident.tile([P, PACK, P], BF16, name="s_sb%d" % i) for i in range(TILES)]
+        v_sb = [resident.tile([P, C, DIMS], BF16, name="v_sb%d" % i) for i in range(TILES)]
+        wv_sb = [resident.tile([P, PACK, C], BF16, name="wv_sb%d" % h) for h in range(PASSES)]
+        gain = const.tile([P, C], BF16)
+
+        def load_point_tile(i):
+            rows = slice(i * P, (i + 1) * P)
+            nc.sync.dma_start(out=g_sb[i][:], in_=g_v[rows, :].rearrange("n (b m) -> n b m", m=P))
+            nc.sync.dma_start(out=s_sb[i][:], in_=s[rows, :].rearrange("n (b m) -> n b m", m=P))
+            nc.sync.dma_start(out=v_sb[i][:], in_=v[rows, :, :])
+
+        load_point_tile(0)
+        for h in range(PASSES):
+            nc.sync.dma_start(
+                out=wv_sb[h][:],
+                in_=wv[h * PACK * P : (h + 1) * PACK * P, :].rearrange("(t p) c -> p t c", p=P),
+            )
+        nc.sync.dma_start(out=gain[:], in_=ln_g1.partition_broadcast(P))
+        for i in range(1, TILES):
+            load_point_tile(i)
+
+        ident = const.tile([P, P], BF16)
+        make_identity(nc, ident[:])
+        one = const.tile([P, 1], F32)
+        nc.vector.memset(one[:], 1.0)
+        nc.scalar.activation(out=one[:], in_=one[:], func=ACT.Sqrt)
+
+        wv_grouped = const.tile([P, PASSES, C, PACK], BF16, align_bytes=64)
+        wv_codes = const.tile([P, PASSES, C], U32, align_bytes=64)
+        wv_scales = const.tile([P, PASSES, C], U8, align_bytes=64)
+
+        def group_wv(h):
+            nc.scalar.copy(
+                out=wv_grouped[:, h].rearrange("p (c i) t -> p c t i", i=4),
+                in_=wv_sb[h][:].rearrange("p t (c i) -> p c t i", i=4),
+            )
+
+        def quantise_wv(h):
+            nc.vector.quantize_mx(
+                out=wv_codes[:, h, :].bitcast(FP8X4),
+                scales=wv_scales[:, h, :],
+                in_=wv_grouped[:, h].rearrange("p c t -> p (c t)"),
+            )
+
+        gT_ps, gT_sb, v2s_ps, v01_ps = {}, {}, {}, {}
+        u01, u2, u01_codes, u01_scales, u2_codes, u2_scales = {}, {}, {}, {}, {}, {}
+        acc, y, y_gain, rms, inv_rms = {}, {}, {}, {}, {}
+
+        def transpose_gates(i):
+            gT_ps[i] = psum_t.tile([P, PASSES, PACK, P], BF16, name="gT_ps", tag="gT_ps")
+            for h in range(PASSES):
+                for t in range(PACK):
+                    nc.tensor.transpose(gT_ps[i][:, h, t, :], g_sb[i][:, h * PACK + t, :], ident[:])
+
+        def copy_gates(i):
+            gT_sb[i] = work.tile([P, PASSES, PACK, P], BF16, name="gT_sb", tag="gT_sb")
+            nc.scalar.copy(out=gT_sb[i][:], in_=gT_ps[i][:])
+
+        def transpose_v2_and_s(i):
+            v2s_ps[i] = psum_t.tile([P, 2, PACK, P], BF16, name="v2s_ps", tag="v2s_ps")
+            for t in range(PACK):
+                nc.tensor.transpose(v2s_ps[i][:, 1, t, :], s_sb[i][:, t, :], ident[:])
+            for t in range(PACK):
+                nc.tensor.transpose(v2s_ps[i][:, 0, t, :], v_sb[i][:, t * P : (t + 1) * P, 2], ident[:])
+
+        def transpose_v01(i):
+            v01_ps[i] = psum_t.tile([P, 2, PACK, P], BF16, name="v01_ps", tag="v01_ps")
+            for d in range(2):
+                for t in range(PACK):
+                    nc.tensor.transpose(v01_ps[i][:, d, t, :], v_sb[i][:, t * P : (t + 1) * P, d], ident[:])
+
+        def products_d2(i):
+            g1 = gT_sb[i][:, 0].rearrange("p t n -> p n t")
+            g2 = gT_sb[i][:, 1].rearrange("p t n -> p n t")
+            sT = v2s_ps[i][:, 1].rearrange("p t n -> p n t")
+            v2T = v2s_ps[i][:, 0].rearrange("p t n -> p n t")
+            sg = work.tile([P, P, PACK], F32, name="sg", tag="sg")
+            nc.vector.scalar_tensor_tensor(out=sg[:], in0=sT, scalar=math.sqrt(2.0), in1=g2, op0=MULT, op1=MULT)
+            u2[i] = work.tile([P, PASSES, P, PACK], BF16, name="u2", tag="u2", align_bytes=64)
+            nc.vector.tensor_tensor(out=u2[i][:, 0], in0=v2T, in1=g1, op=MULT)
+            nc.vector.tensor_tensor(out=u2[i][:, 1], in0=v2T, in1=sg[:], op=MULT)
+            return sg
+
+        def product_d01(i, h, gate):
+            vT = v01_ps[i][:].rearrange("p d t n -> p d n t")
+            nc.vector.tensor_tensor(
+                out=u01[i][:, h], in0=vT, in1=gate.unsqueeze(1).to_broadcast([P, 2, P, PACK]), op=MULT
+            )
+
+        def quantise_d2(i):
+            u2_codes[i] = work.tile([P, PASSES, P], U32, name="u2_codes", tag="u2_codes", align_bytes=64)
+            u2_scales[i] = work.tile([P, PASSES, P], U8, name="u2_scales", tag="u2_scales", align_bytes=64)
+            nc.vector.quantize_mx(
+                out=u2_codes[i][:].rearrange("p h n -> p (h n)").bitcast(FP8X4),
+                scales=u2_scales[i][:].rearrange("p h n -> p (h n)"),
+                in_=u2[i][:].rearrange("p h n t -> p (h n t)"),
+            )
+
+        def quantise_d01(i):
+            u01_codes[i] = work.tile([P, PASSES, 2, P], U32, name="u01_codes", tag="u01_codes", align_bytes=64)
+            u01_scales[i] = work.tile([P, PASSES, 2, P], U8, name="u01_scales", tag="u01_scales", align_bytes=64)
+            nc.vector.quantize_mx(
+                out=u01_codes[i][:].rearrange("p h d n -> p (h d n)").bitcast(FP8X4),
+                scales=u01_scales[i][:].rearrange("p h d n -> p (h d n)"),
+                in_=u01[i][:].rearrange("p h d n t -> p (h d n t)"),
+            )
+
+        def multiply(i, d):
+            acc[i, d] = psum_acc.tile([P, C], F32, name="acc", tag="acc")
+            for h in range(PASSES):
+                codes = u2_codes[i][:, h, :] if d == 2 else u01_codes[i][:, h, d, :]
+                scales = u2_scales[i][:, h, :] if d == 2 else u01_scales[i][:, h, d, :]
+                nc.tensor.matmul_mx(
+                    out=acc[i, d][:],
+                    lhsT=codes.bitcast(FP8X4),
+                    lhsT_scale=scales,
+                    rhs=wv_codes[:, h, :].bitcast(FP8X4),
+                    rhs_scale=wv_scales[:, h, :],
+                    start=(h == 0),
+                    stop=(h == PASSES - 1),
+                )
+
+        def residual(i, d):
+            nc.vector.scalar_tensor_tensor(
+                out=y[i][:, d, :], in0=acc[i, d][:], scalar=1.0 / math.sqrt(PASSES * C),
+                in1=v_sb[i][:, :, d], op0=MULT, op1=ADD,
+            )
+            nc.gpsimd.tensor_tensor(out=y_gain[i][:, d, :], in0=y[i][:, d, :], in1=gain[:], op=MULT)
+
+        def root_mean_square(i):
+            squares = work.tile([P, DIMS * C], F32, name="squares", tag="squares")
+            sum_sq = work.tile([P, 1], F32, name="sum_sq", tag="sum_sq")
+            nc.scalar.activation(
+                out=squares[:], in_=y[i][:].rearrange("p d c -> p (d c)"), func=ACT.Square, accum_out=sum_sq[:]
+            )
+            rms[i] = work.tile([P, 1], F32, name="rms", tag="rms")
+            nc.scalar.activation(out=rms[i][:], in_=sum_sq[:], func=ACT.Sqrt, scale=1.0 / (DIMS * C), bias=EPS)
+
+        def invert_rms(i):
+            inv_rms[i] = work.tile([P, 1], F32, name="inv_rms", tag="inv_rms")
+            nc.vector.reciprocal(out=inv_rms[i][:], in_=rms[i][:])
+
+        def normalise_and_store(i):
+            result = work.tile([P, C, DIMS], F32, name="result", tag="result")
+            nc.scalar.activation(
+                out=result[:], in_=y_gain[i][:].rearrange("p d c -> p c d"), func=ACT.Copy, scale=inv_rms[i][:]
+            )
+            nc.sync.dma_start(out=out[i * P : (i + 1) * P, :, :], in_=result[:])
+
+        transpose_gates(0)
+        copy_gates(0)
+        transpose_v2_and_s(0)
+        transpose_v01(0)
+        for h in range(PASSES):
+            group_wv(h)
+
+        for j in range(TILES + 2):
+            forming, nxt, adding, storing = j, j + 1, j - 1, j - 2
+            if nxt < TILES:
+                transpose_gates(nxt)
+                copy_gates(nxt)
+            if forming < TILES:
+                sg = products_d2(forming)
+                if nxt < TILES:
+                    transpose_v2_and_s(nxt)
+                u01[forming] = work.tile([P, PASSES, 2, P, PACK], BF16, name="u01", tag="u01", align_bytes=64)
+                product_d01(forming, 0, gT_sb[forming][:, 0].rearrange("p t n -> p n t"))
+            if 0 <= storing:
+                invert_rms(storing)
+            if forming < TILES:
+                quantise_d2(forming)
+                product_d01(forming, 1, sg[:])
+                if nxt < TILES:
+                    transpose_v01(nxt)
+            if 0 <= storing:
+                normalise_and_store(storing)
+            if 0 <= adding < TILES:
+                y[adding] = work.tile([P, DIMS, C], F32, name="y", tag="y")
+                y_gain[adding] = work.tile([P, DIMS, C], F32, name="y_gain", tag="y_gain")
+                residual(adding, 2)
+            if forming == 0:
+                for h in range(PASSES):
+                    quantise_wv(h)
+            if forming < TILES:
+                quantise_d01(forming)
+            if 0 <= adding < TILES:
+                residual(adding, 0)
+                residual(adding, 1)
+                root_mean_square(adding)
+            if forming < TILES:
+                for d in (2, 0, 1):
+                    multiply(forming, d)

@@ -21,6 +21,7 @@ DIMS = 3
 PASSES = 2
 TILES = POINTS // P
 EPS = 1e-6
+GROUPS = ((0,), (1, 2))
 
 FLOPS = 2 * POINTS * DIMS * (PASSES * C) * C
 
@@ -32,10 +33,10 @@ def tile_selfinteraction_pb_kernel(tc, s, v, g_v, wv, ln_g1, out):
         resident = ctx.enter_context(tc.tile_pool(name="resident", bufs=1))
         work = ctx.enter_context(tc.tile_pool(name="work", bufs=2))
         psum_t = ctx.enter_context(tc.psum_pool(name="psum_t", bufs=1))
-        psum_acc = ctx.enter_context(tc.psum_pool(name="psum_acc", bufs=5))
+        psum_acc = ctx.enter_context(tc.psum_pool(name="psum_acc", bufs=4))
         ctx.enter_context(tc.manual_schedule())
 
-        g_sb = [resident.tile([P, PASSES * PACK, P], BF16, name="g_sb%d" % i) for i in range(TILES)]
+        g_sb = [resident.tile([P, PASSES, PACK, P], BF16, name="g_sb%d" % i) for i in range(TILES)]
         s_sb = [resident.tile([P, PACK, P], BF16, name="s_sb%d" % i) for i in range(TILES)]
         v_sb = [resident.tile([P, C, DIMS], BF16, name="v_sb%d" % i) for i in range(TILES)]
         wv_sb = [resident.tile([P, PACK, C], BF16, name="wv_sb%d" % h) for h in range(PASSES)]
@@ -43,9 +44,9 @@ def tile_selfinteraction_pb_kernel(tc, s, v, g_v, wv, ln_g1, out):
 
         def load_point_tile(i):
             rows = slice(i * P, (i + 1) * P)
-            nc.sync.dma_start(out=g_sb[i][:], in_=g_v[rows, :].rearrange("n (b m) -> n b m", m=P))
-            nc.sync.dma_start(out=s_sb[i][:], in_=s[rows, :].rearrange("n (b m) -> n b m", m=P))
+            nc.sync.dma_start(out=g_sb[i][:], in_=g_v[rows, :].rearrange("n (h t m) -> n h t m", t=PACK, m=P))
             nc.sync.dma_start(out=v_sb[i][:], in_=v[rows, :, :])
+            nc.sync.dma_start(out=s_sb[i][:], in_=s[rows, :].rearrange("n (t m) -> n t m", m=P))
 
         load_point_tile(0)
         for h in range(PASSES):
@@ -57,21 +58,25 @@ def tile_selfinteraction_pb_kernel(tc, s, v, g_v, wv, ln_g1, out):
         for i in range(1, TILES):
             load_point_tile(i)
 
-        ident = const.tile([P, P], BF16)
-        make_identity(nc, ident[:])
+        ident_bf16 = const.tile([P, P], BF16)
+        make_identity(nc, ident_bf16[:])
+        ident_f32 = const.tile([P, P], F32)
+        make_identity(nc, ident_f32[:])
         one = const.tile([P, 1], F32)
         nc.vector.memset(one[:], 1.0)
-        nc.scalar.activation(out=one[:], in_=one[:], func=ACT.Sqrt)
+        nc.scalar.activation(out=one[:], in_=one[:], func=ACT.Abs_reciprocal_sqrt)
 
         wv_grouped = const.tile([P, PASSES, C, PACK], BF16, align_bytes=64)
         wv_codes = const.tile([P, PASSES, C], U32, align_bytes=64)
         wv_scales = const.tile([P, PASSES, C], U8, align_bytes=64)
 
         def group_wv(h):
-            nc.scalar.copy(
-                out=wv_grouped[:, h].rearrange("p (c i) t -> p c t i", i=4),
-                in_=wv_sb[h][:].rearrange("p t (c i) -> p c t i", i=4),
-            )
+            dst = wv_grouped[:, h].rearrange("p (c i) t -> p c t i", i=4)
+            src = wv_sb[h][:].rearrange("p t (c i) -> p c t i", i=4)
+            if h == 0:
+                nc.scalar.copy(out=dst, in_=src)
+            else:
+                nc.gpsimd.tensor_scalar(out=dst, in0=src, scalar1=1.0, scalar2=0.0, op0=MULT, op1=ADD)
 
         def quantise_wv(h):
             nc.vector.quantize_mx(
@@ -80,151 +85,164 @@ def tile_selfinteraction_pb_kernel(tc, s, v, g_v, wv, ln_g1, out):
                 in_=wv_grouped[:, h].rearrange("p c t -> p (c t)"),
             )
 
-        gT_ps, gT_sb, v2s_ps, v01_ps = {}, {}, {}, {}
-        u01, u2, u01_codes, u01_scales, u2_codes, u2_scales = {}, {}, {}, {}, {}, {}
-        acc, y, y_gain, rms, inv_rms = {}, {}, {}, {}, {}
+        sg_nat, g1T_ps, sgT_ps, g1T, sgT, vT_ps = {}, {}, {}, {}, {}, {}
+        u, u_codes, u_scales = {}, {}, {}
+        acc, y, y_gain, mean_sq, inv_rms = {}, {}, {}, {}, {}
 
-        def transpose_gates(i):
-            gT_ps[i] = psum_t.tile([P, PASSES, PACK, P], BF16, name="gT_ps", tag="gT_ps")
-            for h in range(PASSES):
-                for t in range(PACK):
-                    nc.tensor.transpose(gT_ps[i][:, h, t, :], g_sb[i][:, h * PACK + t, :], ident[:])
+        def second_gate(i):
+            sg_nat[i] = work.tile([P, PACK, P], F32, name="sg_nat", tag="sg_nat", bufs=3)
+            nc.gpsimd.tensor_tensor(out=sg_nat[i][:], in0=s_sb[i][:], in1=g_sb[i][:, 1], op=MULT)
 
-        def copy_gates(i):
-            gT_sb[i] = work.tile([P, PASSES, PACK, P], BF16, name="gT_sb", tag="gT_sb")
-            nc.scalar.copy(out=gT_sb[i][:], in_=gT_ps[i][:])
-
-        def transpose_v2_and_s(i):
-            v2s_ps[i] = psum_t.tile([P, 2, PACK, P], BF16, name="v2s_ps", tag="v2s_ps")
+        def transpose_first_gate(i):
+            g1T_ps[i] = psum_t.tile([P, PACK, P], BF16, name="g1T_ps", tag="g1T_ps")
             for t in range(PACK):
-                nc.tensor.transpose(v2s_ps[i][:, 1, t, :], s_sb[i][:, t, :], ident[:])
+                nc.tensor.transpose(g1T_ps[i][:, t, :], g_sb[i][:, 0, t, :], ident_bf16[:])
+
+        def transpose_second_gate(i):
+            sgT_ps[i] = psum_t.tile([P, PACK, P], F32, name="sgT_ps", tag="sgT_ps")
             for t in range(PACK):
-                nc.tensor.transpose(v2s_ps[i][:, 0, t, :], v_sb[i][:, t * P : (t + 1) * P, 2], ident[:])
+                nc.tensor.transpose(sgT_ps[i][:, t, :], sg_nat[i][:, t, :], ident_f32[:])
 
-        def transpose_v01(i):
-            v01_ps[i] = psum_t.tile([P, 2, PACK, P], BF16, name="v01_ps", tag="v01_ps")
-            for d in range(2):
+        def copy_first_gate(i):
+            g1T[i] = work.tile([P, P, PACK], BF16, name="g1T", tag="g1T")
+            nc.scalar.copy(out=g1T[i][:], in_=g1T_ps[i][:].rearrange("p t n -> p n t"))
+
+        def copy_second_gate(i):
+            sgT[i] = work.tile([P, P, PACK], F32, name="sgT", tag="sgT")
+            nc.scalar.mul(out=sgT[i][:], in_=sgT_ps[i][:].rearrange("p t n -> p n t"), mul=math.sqrt(2.0))
+
+        def transpose_v(i, k):
+            vT_ps[i, k] = psum_t.tile([P, len(GROUPS[k]), PACK, P], BF16, name="vT_ps%d" % k, tag="vT_ps%d" % k)
+            for e, d in enumerate(GROUPS[k]):
                 for t in range(PACK):
-                    nc.tensor.transpose(v01_ps[i][:, d, t, :], v_sb[i][:, t * P : (t + 1) * P, d], ident[:])
+                    nc.tensor.transpose(vT_ps[i, k][:, e, t, :], v_sb[i][:, t * P : (t + 1) * P, d], ident_bf16[:])
 
-        def products_d2(i):
-            g1 = gT_sb[i][:, 0].rearrange("p t n -> p n t")
-            g2 = gT_sb[i][:, 1].rearrange("p t n -> p n t")
-            sT = v2s_ps[i][:, 1].rearrange("p t n -> p n t")
-            v2T = v2s_ps[i][:, 0].rearrange("p t n -> p n t")
-            sg = work.tile([P, P, PACK], F32, name="sg", tag="sg")
-            nc.vector.scalar_tensor_tensor(out=sg[:], in0=sT, scalar=math.sqrt(2.0), in1=g2, op0=MULT, op1=MULT)
-            u2[i] = work.tile([P, PASSES, P, PACK], BF16, name="u2", tag="u2", align_bytes=64)
-            nc.vector.tensor_tensor(out=u2[i][:, 0], in0=v2T, in1=g1, op=MULT)
-            nc.vector.tensor_tensor(out=u2[i][:, 1], in0=v2T, in1=sg[:], op=MULT)
-            return sg
-
-        def product_d01(i, h, gate):
-            vT = v01_ps[i][:].rearrange("p d t n -> p d n t")
-            nc.vector.tensor_tensor(
-                out=u01[i][:, h], in0=vT, in1=gate.unsqueeze(1).to_broadcast([P, 2, P, PACK]), op=MULT
-            )
-
-        def quantise_d2(i):
-            u2_codes[i] = work.tile([P, PASSES, P], U32, name="u2_codes", tag="u2_codes", align_bytes=64)
-            u2_scales[i] = work.tile([P, PASSES, P], U8, name="u2_scales", tag="u2_scales", align_bytes=64)
-            nc.vector.quantize_mx(
-                out=u2_codes[i][:].rearrange("p h n -> p (h n)").bitcast(FP8X4),
-                scales=u2_scales[i][:].rearrange("p h n -> p (h n)"),
-                in_=u2[i][:].rearrange("p h n t -> p (h n t)"),
-            )
-
-        def quantise_d01(i):
-            u01_codes[i] = work.tile([P, PASSES, 2, P], U32, name="u01_codes", tag="u01_codes", align_bytes=64)
-            u01_scales[i] = work.tile([P, PASSES, 2, P], U8, name="u01_scales", tag="u01_scales", align_bytes=64)
-            nc.vector.quantize_mx(
-                out=u01_codes[i][:].rearrange("p h d n -> p (h d n)").bitcast(FP8X4),
-                scales=u01_scales[i][:].rearrange("p h d n -> p (h d n)"),
-                in_=u01[i][:].rearrange("p h d n t -> p (h d n t)"),
-            )
-
-        def multiply(i, d):
-            acc[i, d] = psum_acc.tile([P, C], F32, name="acc", tag="acc")
-            for h in range(PASSES):
-                codes = u2_codes[i][:, h, :] if d == 2 else u01_codes[i][:, h, d, :]
-                scales = u2_scales[i][:, h, :] if d == 2 else u01_scales[i][:, h, d, :]
-                nc.tensor.matmul_mx(
-                    out=acc[i, d][:],
-                    lhsT=codes.bitcast(FP8X4),
-                    lhsT_scale=scales,
-                    rhs=wv_codes[:, h, :].bitcast(FP8X4),
-                    rhs_scale=wv_scales[:, h, :],
-                    start=(h == 0),
-                    stop=(h == PASSES - 1),
+        def product(i, k, h, gate):
+            if h == 0:
+                u[i, k] = work.tile(
+                    [P, PASSES, len(GROUPS[k]), P, PACK], BF16, name="u%d" % k, tag="u%d" % k, align_bytes=64
                 )
+            nc.vector.tensor_tensor(
+                out=u[i, k][:, h],
+                in0=vT_ps[i, k][:].rearrange("p e t n -> p e n t"),
+                in1=gate[:].unsqueeze(1).to_broadcast([P, len(GROUPS[k]), P, PACK]),
+                op=MULT,
+            )
+
+        def quantise(i, k):
+            shape = [P, PASSES, len(GROUPS[k]), P]
+            u_codes[i, k] = work.tile(shape, U32, name="u_codes%d" % k, tag="u_codes%d" % k, align_bytes=64)
+            u_scales[i, k] = work.tile(shape, U8, name="u_scales%d" % k, tag="u_scales%d" % k, align_bytes=64)
+            nc.vector.quantize_mx(
+                out=u_codes[i, k][:].rearrange("p h e n -> p (h e n)").bitcast(FP8X4),
+                scales=u_scales[i, k][:].rearrange("p h e n -> p (h e n)"),
+                in_=u[i, k][:].rearrange("p h e n t -> p (h e n t)"),
+            )
+
+        def multiply(i, k):
+            for e, d in enumerate(GROUPS[k]):
+                acc[i, d] = psum_acc.tile([P, C], F32, name="acc", tag="acc")
+                for h in range(PASSES):
+                    nc.tensor.matmul_mx(
+                        out=acc[i, d][:],
+                        lhsT=u_codes[i, k][:, h, e, :].bitcast(FP8X4),
+                        lhsT_scale=u_scales[i, k][:, h, e, :],
+                        rhs=wv_codes[:, h, :].bitcast(FP8X4),
+                        rhs_scale=wv_scales[:, h, :],
+                        start=(h == 0),
+                        stop=(h == PASSES - 1),
+                    )
 
         def residual(i, d):
+            if d == 0:
+                y[i] = work.tile([P, DIMS, C], F32, name="y", tag="y")
+                y_gain[i] = work.tile([P, DIMS, C], F32, name="y_gain", tag="y_gain")
             nc.vector.scalar_tensor_tensor(
                 out=y[i][:, d, :], in0=acc[i, d][:], scalar=1.0 / math.sqrt(PASSES * C),
                 in1=v_sb[i][:, :, d], op0=MULT, op1=ADD,
             )
             nc.gpsimd.tensor_tensor(out=y_gain[i][:, d, :], in0=y[i][:, d, :], in1=gain[:], op=MULT)
 
-        def root_mean_square(i):
-            squares = work.tile([P, DIMS * C], F32, name="squares", tag="squares")
-            sum_sq = work.tile([P, 1], F32, name="sum_sq", tag="sum_sq")
+        def mean_square(i, first, last):
+            squares = work.tile([P, DIMS, C], F32, name="squares", tag="squares")
+            share = work.tile([P, 1], F32, name="share", tag="share", bufs=4)
             nc.scalar.activation(
-                out=squares[:], in_=y[i][:].rearrange("p d c -> p (d c)"), func=ACT.Square, accum_out=sum_sq[:]
+                out=squares[:, first:last, :], in_=y[i][:, first:last, :], func=ACT.Square,
+                scale=1.0 / math.sqrt(DIMS * C), accum_out=share[:],
             )
-            rms[i] = work.tile([P, 1], F32, name="rms", tag="rms")
-            nc.scalar.activation(out=rms[i][:], in_=sum_sq[:], func=ACT.Sqrt, scale=1.0 / (DIMS * C), bias=EPS)
+            return share
 
-        def invert_rms(i):
+        def mean_square_of_two(i):
+            share = mean_square(i, 0, 2)
+            mean_sq[i] = work.tile([P, 1], F32, name="mean_sq", tag="mean_sq")
+            nc.scalar.activation(out=mean_sq[i][:], in_=share[:], func=ACT.Copy, bias=EPS)
+
+        def inverse_rms(i):
+            share = mean_square(i, 2, DIMS)
             inv_rms[i] = work.tile([P, 1], F32, name="inv_rms", tag="inv_rms")
-            nc.vector.reciprocal(out=inv_rms[i][:], in_=rms[i][:])
+            nc.scalar.activation(
+                out=inv_rms[i][:], in_=share[:], func=ACT.Abs_reciprocal_sqrt, bias=mean_sq[i][:]
+            )
 
         def normalise_and_store(i):
-            result = work.tile([P, C, DIMS], F32, name="result", tag="result")
-            nc.scalar.activation(
-                out=result[:], in_=y_gain[i][:].rearrange("p d c -> p c d"), func=ACT.Copy, scale=inv_rms[i][:]
-            )
-            nc.sync.dma_start(out=out[i * P : (i + 1) * P, :, :], in_=result[:])
+            for half in range(2):
+                cols = slice(half * C // 2, (half + 1) * C // 2)
+                result = work.tile([P, C // 2, DIMS], F32, name="result", tag="result", bufs=4)
+                nc.scalar.activation(
+                    out=result[:], in_=y_gain[i][:, :, cols].rearrange("p d c -> p c d"),
+                    func=ACT.Copy, scale=inv_rms[i][:],
+                )
+                nc.sync.dma_start(out=out[i * P : (i + 1) * P, cols, :], in_=result[:])
 
-        transpose_gates(0)
-        copy_gates(0)
-        transpose_v2_and_s(0)
-        transpose_v01(0)
+        second_gate(0)
+        transpose_first_gate(0)
+        copy_first_gate(0)
+        transpose_v(0, 0)
+        transpose_v(0, 1)
+        transpose_second_gate(0)
+        copy_second_gate(0)
         for h in range(PASSES):
             group_wv(h)
+        second_gate(1)
 
         for j in range(TILES + 2):
-            forming, nxt, adding, storing = j, j + 1, j - 1, j - 2
-            if nxt < TILES:
-                transpose_gates(nxt)
-                copy_gates(nxt)
-            if forming < TILES:
-                sg = products_d2(forming)
-                if nxt < TILES:
-                    transpose_v2_and_s(nxt)
-                u01[forming] = work.tile([P, PASSES, 2, P, PACK], BF16, name="u01", tag="u01", align_bytes=64)
-                product_d01(forming, 0, gT_sb[forming][:, 0].rearrange("p t n -> p n t"))
-            if 0 <= storing:
-                invert_rms(storing)
-            if forming < TILES:
-                quantise_d2(forming)
-                product_d01(forming, 1, sg[:])
-                if nxt < TILES:
-                    transpose_v01(nxt)
-            if 0 <= storing:
-                normalise_and_store(storing)
-            if 0 <= adding < TILES:
-                y[adding] = work.tile([P, DIMS, C], F32, name="y", tag="y")
-                y_gain[adding] = work.tile([P, DIMS, C], F32, name="y_gain", tag="y_gain")
-                residual(adding, 2)
-            if forming == 0:
-                for h in range(PASSES):
-                    quantise_wv(h)
-            if forming < TILES:
-                quantise_d01(forming)
-            if 0 <= adding < TILES:
-                residual(adding, 0)
-                residual(adding, 1)
-                root_mean_square(adding)
-            if forming < TILES:
-                for d in (2, 0, 1):
-                    multiply(forming, d)
+            forming = j < TILES
+            preparing = j + 1 < TILES
+            adding = 0 <= j - 1 < TILES
+            storing = 0 <= j - 2
+            if j + 2 < TILES:
+                second_gate(j + 2)
+            if preparing:
+                transpose_first_gate(j + 1)
+                transpose_second_gate(j + 1)
+                copy_first_gate(j + 1)
+                copy_second_gate(j + 1)
+            if storing:
+                normalise_and_store(j - 2)
+            if forming:
+                product(j, 0, 0, g1T[j])
+                product(j, 1, 0, g1T[j])
+                product(j, 0, 1, sgT[j])
+            if preparing:
+                transpose_v(j + 1, 0)
+            if adding:
+                residual(j - 1, 0)
+            if forming:
+                quantise(j, 0)
+                product(j, 1, 1, sgT[j])
+                if j == 0:
+                    for h in range(PASSES):
+                        quantise_wv(h)
+                multiply(j, 0)
+            if preparing:
+                transpose_v(j + 1, 1)
+            if adding:
+                residual(j - 1, 1)
+                mean_square_of_two(j - 1)
+            if forming:
+                quantise(j, 1)
+            if adding:
+                residual(j - 1, 2)
+                inverse_rms(j - 1)
+            if forming:
+                multiply(j, 1)

@@ -90,7 +90,7 @@ def tile_selfinteraction_pb_kernel(tc, s, v, g_v, wv, ln_g1, out):
         acc, y, y_gain, mean_sq, inv_rms = {}, {}, {}, {}, {}
 
         def second_gate(i):
-            sg_nat[i] = work.tile([P, PACK, P], F32, name="sg_nat", tag="sg_nat", bufs=3)
+            sg_nat[i] = resident.tile([P, PACK, P], F32, name="sg_nat%d" % i)
             nc.gpsimd.tensor_tensor(out=sg_nat[i][:], in0=s_sb[i][:], in1=g_sb[i][:, 1], op=MULT)
 
         def transpose_first_gate(i):
@@ -203,15 +203,14 @@ def tile_selfinteraction_pb_kernel(tc, s, v, g_v, wv, ln_g1, out):
         copy_second_gate(0)
         for h in range(PASSES):
             group_wv(h)
-        second_gate(1)
+        for i in range(1, TILES):
+            second_gate(i)
 
         for j in range(TILES + 2):
             forming = j < TILES
             preparing = j + 1 < TILES
             adding = 0 <= j - 1 < TILES
             storing = 0 <= j - 2
-            if j + 2 < TILES:
-                second_gate(j + 2)
             if preparing:
                 transpose_first_gate(j + 1)
                 transpose_second_gate(j + 1)
@@ -225,24 +224,23 @@ def tile_selfinteraction_pb_kernel(tc, s, v, g_v, wv, ln_g1, out):
                 product(j, 0, 1, sgT[j])
             if preparing:
                 transpose_v(j + 1, 0)
-            if adding:
-                residual(j - 1, 0)
+            if forming:
+                product(j, 1, 1, sgT[j])
+            if preparing:
+                transpose_v(j + 1, 1)
             if forming:
                 quantise(j, 0)
-                product(j, 1, 1, sgT[j])
                 if j == 0:
                     for h in range(PASSES):
                         quantise_wv(h)
+                quantise(j, 1)
                 multiply(j, 0)
-            if preparing:
-                transpose_v(j + 1, 1)
             if adding:
+                residual(j - 1, 0)
                 residual(j - 1, 1)
                 mean_square_of_two(j - 1)
             if forming:
-                quantise(j, 1)
+                multiply(j, 1)
             if adding:
                 residual(j - 1, 2)
                 inverse_rms(j - 1)
-            if forming:
-                multiply(j, 1)

from contextlib import ExitStack
import math

import concourse.mybir as mybir
from concourse.masks import make_identity

BF16 = mybir.dt.bfloat16
F32 = mybir.dt.float32
U32 = mybir.dt.uint32
U8 = mybir.dt.uint8
FP8X4 = mybir.dt.float8_e4m3fn_x4
MULT = mybir.AluOpType.mult
ADD = mybir.AluOpType.add
ACT = mybir.ActivationFunctionType

P = 128
PACK = 4
POINTS = 768
C = 512
DIMS = 3
PASSES = 2
TILES = POINTS // P
EPS = 1e-6
GROUPS = ((0,), (1, 2))

FLOPS = 2 * POINTS * DIMS * (PASSES * C) * C


def tile_selfinteraction_pb_kernel(tc, s, v, g_v, wv, ln_g1, out):
    nc = tc.nc
    with ExitStack() as ctx:
        const = ctx.enter_context(tc.tile_pool(name="const", bufs=1))
        resident = ctx.enter_context(tc.tile_pool(name="resident", bufs=1))
        work = ctx.enter_context(tc.tile_pool(name="work", bufs=2))
        psum_t = ctx.enter_context(tc.psum_pool(name="psum_t", bufs=1))
        psum_acc = ctx.enter_context(tc.psum_pool(name="psum_acc", bufs=4))
        ctx.enter_context(tc.manual_schedule())

        g_sb = [resident.tile([P, PASSES, PACK, P], BF16, name="g_sb%d" % i) for i in range(TILES)]
        s_sb = [resident.tile([P, PACK, P], BF16, name="s_sb%d" % i) for i in range(TILES)]
        v_sb = [resident.tile([P, C, DIMS], BF16, name="v_sb%d" % i) for i in range(TILES)]
        wv_sb = [resident.tile([P, PACK, C], BF16, name="wv_sb%d" % h) for h in range(PASSES)]
        gain = const.tile([P, C], BF16)

        def load_point_tile(i):
            rows = slice(i * P, (i + 1) * P)
            nc.sync.dma_start(out=g_sb[i][:], in_=g_v[rows, :].rearrange("n (h t m) -> n h t m", t=PACK, m=P))
            nc.sync.dma_start(out=v_sb[i][:], in_=v[rows, :, :])
            nc.sync.dma_start(out=s_sb[i][:], in_=s[rows, :].rearrange("n (t m) -> n t m", m=P))

        load_point_tile(0)
        for h in range(PASSES):
            nc.sync.dma_start(
                out=wv_sb[h][:],
                in_=wv[h * PACK * P : (h + 1) * PACK * P, :].rearrange("(t p) c -> p t c", p=P),
            )
        nc.sync.dma_start(out=gain[:], in_=ln_g1.partition_broadcast(P))
        for i in range(1, TILES):
            load_point_tile(i)

        ident_bf16 = const.tile([P, P], BF16)
        make_identity(nc, ident_bf16[:])
        ident_f32 = const.tile([P, P], F32)
        make_identity(nc, ident_f32[:])
        one = const.tile([P, 1], F32)
        nc.vector.memset(one[:], 1.0)
        nc.scalar.activation(out=one[:], in_=one[:], func=ACT.Abs_reciprocal_sqrt)

        wv_grouped = const.tile([P, PASSES, C, PACK], BF16, align_bytes=64)
        wv_codes = const.tile([P, PASSES, C], U32, align_bytes=64)
        wv_scales = const.tile([P, PASSES, C], U8, align_bytes=64)

        def group_wv(h):
            dst = wv_grouped[:, h].rearrange("p (c i) t -> p c t i", i=4)
            src = wv_sb[h][:].rearrange("p t (c i) -> p c t i", i=4)
            if h == 0:
                nc.scalar.copy(out=dst, in_=src)
            else:
                nc.gpsimd.tensor_scalar(out=dst, in0=src, scalar1=1.0, scalar2=0.0, op0=MULT, op1=ADD)

        def quantise_wv(h):
            nc.vector.quantize_mx(
                out=wv_codes[:, h, :].bitcast(FP8X4),
                scales=wv_scales[:, h, :],
                in_=wv_grouped[:, h].rearrange("p c t -> p (c t)"),
            )

        sg_nat, g1T_ps, sgT_ps, g1T, sgT, vT_ps = {}, {}, {}, {}, {}, {}
        u, u_codes, u_scales = {}, {}, {}
        acc, y, y_gain, mean_sq, inv_rms = {}, {}, {}, {}, {}

        def second_gate(i):
            sg_nat[i] = resident.tile([P, PACK, P], F32, name="sg_nat%d" % i)
            nc.gpsimd.tensor_tensor(out=sg_nat[i][:], in0=s_sb[i][:], in1=g_sb[i][:, 1], op=MULT)

        def transpose_first_gate(i):
            g1T_ps[i] = psum_t.tile([P, PACK, P], BF16, name="g1T_ps", tag="g1T_ps")
            for t in range(PACK):
                nc.tensor.transpose(g1T_ps[i][:, t, :], g_sb[i][:, 0, t, :], ident_bf16[:])

        def transpose_second_gate(i):
            sgT_ps[i] = psum_t.tile([P, PACK, P], F32, name="sgT_ps", tag="sgT_ps")
            for t in range(PACK):
                nc.tensor.transpose(sgT_ps[i][:, t, :], sg_nat[i][:, t, :], ident_f32[:])

        def copy_first_gate(i):
            g1T[i] = work.tile([P, P, PACK], BF16, name="g1T", tag="g1T")
            nc.scalar.copy(out=g1T[i][:], in_=g1T_ps[i][:].rearrange("p t n -> p n t"))

        def copy_second_gate(i):
            sgT[i] = work.tile([P, P, PACK], F32, name="sgT", tag="sgT")
            nc.scalar.mul(out=sgT[i][:], in_=sgT_ps[i][:].rearrange("p t n -> p n t"), mul=math.sqrt(2.0))

        def transpose_v(i, k):
            vT_ps[i, k] = psum_t.tile([P, len(GROUPS[k]), PACK, P], BF16, name="vT_ps%d" % k, tag="vT_ps%d" % k)
            for e, d in enumerate(GROUPS[k]):
                for t in range(PACK):
                    nc.tensor.transpose(vT_ps[i, k][:, e, t, :], v_sb[i][:, t * P : (t + 1) * P, d], ident_bf16[:])

        def product(i, k, h, gate):
            if h == 0:
                u[i, k] = work.tile(
                    [P, PASSES, len(GROUPS[k]), P, PACK], BF16, name="u%d" % k, tag="u%d" % k, align_bytes=64
                )
            nc.vector.tensor_tensor(
                out=u[i, k][:, h],
                in0=vT_ps[i, k][:].rearrange("p e t n -> p e n t"),
                in1=gate[:].unsqueeze(1).to_broadcast([P, len(GROUPS[k]), P, PACK]),
                op=MULT,
            )

        def quantise(i, k):
            shape = [P, PASSES, len(GROUPS[k]), P]
            u_codes[i, k] = work.tile(shape, U32, name="u_codes%d" % k, tag="u_codes%d" % k, align_bytes=64)
            u_scales[i, k] = work.tile(shape, U8, name="u_scales%d" % k, tag="u_scales%d" % k, align_bytes=64)
            nc.vector.quantize_mx(
                out=u_codes[i, k][:].rearrange("p h e n -> p (h e n)").bitcast(FP8X4),
                scales=u_scales[i, k][:].rearrange("p h e n -> p (h e n)"),
                in_=u[i, k][:].rearrange("p h e n t -> p (h e n t)"),
            )

        def multiply(i, k):
            for e, d in enumerate(GROUPS[k]):
                acc[i, d] = psum_acc.tile([P, C], F32, name="acc", tag="acc")
                for h in range(PASSES):
                    nc.tensor.matmul_mx(
                        out=acc[i, d][:],
                        lhsT=u_codes[i, k][:, h, e, :].bitcast(FP8X4),
                        lhsT_scale=u_scales[i, k][:, h, e, :],
                        rhs=wv_codes[:, h, :].bitcast(FP8X4),
                        rhs_scale=wv_scales[:, h, :],
                        start=(h == 0),
                        stop=(h == PASSES - 1),
                    )

        def residual(i, d):
            if d == 0:
                y[i] = work.tile([P, DIMS, C], F32, name="y", tag="y")
                y_gain[i] = work.tile([P, DIMS, C], F32, name="y_gain", tag="y_gain")
            nc.vector.scalar_tensor_tensor(
                out=y[i][:, d, :], in0=acc[i, d][:], scalar=1.0 / math.sqrt(PASSES * C),
                in1=v_sb[i][:, :, d], op0=MULT, op1=ADD,
            )
            nc.gpsimd.tensor_tensor(out=y_gain[i][:, d, :], in0=y[i][:, d, :], in1=gain[:], op=MULT)

        def mean_square(i, first, last):
            squares = work.tile([P, DIMS, C], F32, name="squares", tag="squares")
            share = work.tile([P, 1], F32, name="share", tag="share", bufs=4)
            nc.scalar.activation(
                out=squares[:, first:last, :], in_=y[i][:, first:last, :], func=ACT.Square,
                scale=1.0 / math.sqrt(DIMS * C), accum_out=share[:],
            )
            return share

        def mean_square_of_two(i):
            share = mean_square(i, 0, 2)
            mean_sq[i] = work.tile([P, 1], F32, name="mean_sq", tag="mean_sq")
            nc.scalar.activation(out=mean_sq[i][:], in_=share[:], func=ACT.Copy, bias=EPS)

        def inverse_rms(i):
            share = mean_square(i, 2, DIMS)
            inv_rms[i] = work.tile([P, 1], F32, name="inv_rms", tag="inv_rms")
            nc.scalar.activation(
                out=inv_rms[i][:], in_=share[:], func=ACT.Abs_reciprocal_sqrt, bias=mean_sq[i][:]
            )

        def normalise_and_store(i):
            for half in range(2):
                cols = slice(half * C // 2, (half + 1) * C // 2)
                result = work.tile([P, C // 2, DIMS], F32, name="result", tag="result", bufs=4)
                nc.scalar.activation(
                    out=result[:], in_=y_gain[i][:, :, cols].rearrange("p d c -> p c d"),
                    func=ACT.Copy, scale=inv_rms[i][:],
                )
                nc.sync.dma_start(out=out[i * P : (i + 1) * P, cols, :], in_=result[:])

        second_gate(0)
        transpose_first_gate(0)
        copy_first_gate(0)
        transpose_v(0, 0)
        transpose_v(0, 1)
        transpose_second_gate(0)
        copy_second_gate(0)
        for h in range(PASSES):
            group_wv(h)
        for i in range(1, TILES):
            second_gate(i)

        for j in range(TILES + 2):
            forming = j < TILES
            preparing = j + 1 < TILES
            adding = 0 <= j - 1 < TILES
            storing = 0 <= j - 2
            if preparing:
                transpose_first_gate(j + 1)
                transpose_second_gate(j + 1)
                copy_first_gate(j + 1)
                copy_second_gate(j + 1)
            if storing:
                normalise_and_store(j - 2)
            if forming:
                product(j, 0, 0, g1T[j])
                product(j, 1, 0, g1T[j])
                product(j, 0, 1, sgT[j])
            if preparing:
                transpose_v(j + 1, 0)
            if forming:
                product(j, 1, 1, sgT[j])
            if preparing:
                transpose_v(j + 1, 1)
            if forming:
                quantise(j, 0)
                if j == 0:
                    for h in range(PASSES):
                        quantise_wv(h)
                quantise(j, 1)
                multiply(j, 0)
            if adding:
                residual(j - 1, 0)
                residual(j - 1, 1)
                mean_square_of_two(j - 1)
            if forming:
                multiply(j, 1)
            if adding:
                residual(j - 1, 2)
                inverse_rms(j - 1)
